import numpy as np
import ml_dtypes


def mxq(x, axis, fmt="e4m3"):
    dtype, down = {"e4m3": (ml_dtypes.float8_e4m3fn, 7), "e5m2": (ml_dtypes.float8_e5m2, 14)}[fmt]
    v = np.moveaxis(np.asarray(x, np.float32).astype(ml_dtypes.bfloat16).astype(np.float64), axis, -1)
    blocks = v.reshape(v.shape[:-1] + (-1, 32))
    amax = np.abs(blocks).max(-1, keepdims=True)
    byte = np.maximum(np.where(amax > 0, np.frexp(amax)[1] - 1 + 127, 0) - down, 1)
    scale = np.exp2(byte - 127.0)
    codes = (blocks / scale).astype(np.float32).astype(dtype).astype(np.float64)
    return np.moveaxis((codes * scale).reshape(v.shape), -1, axis)


WIDE = False


def mx_kscale(k):
    if not WIDE:
        return np.ones(k)
    levels = np.array([10, -10, 5, -5, 0])
    if k % 512:
        return np.exp2(np.random.permutation(np.resize(levels, k // 32))).repeat(32)
    a = np.empty((k // 512, 16))
    for p in range(k // 512):
        a[p, :8] = np.random.permutation(np.resize(levels, 8))
        for g in range(8):
            far = levels[np.abs(levels - a[p, g]) >= 10]
            a[p, g + 8] = far[np.random.randint(len(far))]
    return np.exp2(a.ravel()).repeat(32)


BF16 = ml_dtypes.bfloat16


def bf(x):
    return np.asarray(x, np.float32).astype(BF16)


def f64(x):
    return np.asarray(x).astype(np.float64)


B, N, L, H, S, R, C = 4, 1024, 4, 64, 2, 2, 512
M = R * S * H
BN_EPS = 1e-5


def setup_inputs():
    s = mx_kscale(L * M).reshape(L, M)
    t = mx_kscale(C)
    return {"hops": bf((1.7 * np.random.standard_normal((B, N, L, M)) + 0.4 * np.random.standard_normal((L, M))) * s),
            "weight": bf(np.random.standard_normal((L, M, C)) * 0.6 / np.sqrt(L * M) / s[:, :, None]),
            "gamma": bf((1.0 + 0.1 * np.random.standard_normal(C)) * t),
            "beta": bf(0.2 * np.random.standard_normal(C) * t),
            "w2": bf(np.random.standard_normal((C, C)) / np.sqrt(C) / t[None, :]),
            "b2": bf(0.2 * np.random.standard_normal(C))}


def reference(hops, weight, gamma, beta, w2, b2):
    hf = f64(hops).reshape(B * N, L * M)
    wm = f64(weight).reshape(L * M, C)
    flat = mxq(hf, 1, "e4m3") @ mxq(wm, 0, "e4m3")
    mean = flat.mean(axis=0)
    var = flat.var(axis=0)
    normed = (flat - mean) * (1.0 / np.sqrt(var + BN_EPS)) * f64(gamma) + f64(beta)
    y = np.maximum(normed, 0.0)
    out = (mxq(y, 1, "e4m3") @ mxq(f64(w2), 1, "e4m3").T) + f64(b2)
    return out.reshape(B, N, C)

@@ -1,0 +1,343 @@
+from contextlib import ExitStack
+
+import concourse.mybir as mybir
+from concourse.masks import make_identity
+
+F32 = mybir.dt.float32
+BF16 = mybir.dt.bfloat16
+U32 = mybir.dt.uint32
+U8 = mybir.dt.uint8
+FP8X4 = mybir.dt.float8_e4m3fn_x4
+ACT = mybir.ActivationFunctionType
+ALU = mybir.AluOpType
+
+P = 128
+ROWS = 4096
+K1 = 1024
+C = 512
+GROUP = 512
+NG = ROWS // GROUP
+IN_PSUM = (6, 7)
+COPIED = (0, 1)
+BN_EPS = 1e-5
+FLOPS = 2 * ROWS * K1 * C + 2 * ROWS * C * C
+V_BLOCKS = 96
+USE_ARS = True
+S_FROM = 3
+
+
+def tile_ginconvfft_pb_t_kernel(tc, hops, weight, gamma, beta, w2, b2, out):
+    nc = tc.nc
+    hflat = hops.rearrange("b n l m -> (b n) (l m)")
+    wflat = weight.rearrange("l m c -> (l m) c")
+    oflat = out.rearrange("b n o -> (b n) o")
+
+    with ExitStack() as ctx:
+        consts = ctx.enter_context(tc.tile_pool(name="consts", bufs=1))
+        raws = ctx.enter_context(tc.tile_pool(name="raws", bufs=5))
+        grps = ctx.enter_context(tc.tile_pool(name="grps", bufs=3))
+        hq = ctx.enter_context(tc.tile_pool(name="hq", bufs=1))
+        zpool = ctx.enter_context(tc.tile_pool(name="zpool", bufs=1))
+        ypool = ctx.enter_context(tc.tile_pool(name="ypool", bufs=3))
+        opool = ctx.enter_context(tc.tile_pool(name="opool", bufs=3))
+        psum = ctx.enter_context(tc.psum_pool(name="psum", bufs=4))
+
+        eps = consts.tile([P, 1], F32, name="eps")
+        nc.vector.memset(eps[:], BN_EPS)
+        junk = consts.tile([P, 1], F32, name="junk")
+        ident_f = consts.tile([P, P], F32, name="ident_f")
+        make_identity(nc, ident_f[:])
+
+        wraw = raws.tile([P, 4096], BF16, name="wraw", tag="raw")
+        wview = wflat.rearrange("(a p e) c -> p a (e c)", a=2, p=P, e=4)
+        for g2 in range(2):
+            nc.sync.dma_start(out=wraw[:, g2 * 2048 : (g2 + 1) * 2048], in_=wview[:, g2, :])
+        hraw = []
+
+        def load_group(g):
+            t = raws.tile([P, 4096], BF16, name="hraw%d" % g, tag="raw")
+            src = hflat[g * GROUP : (g + 1) * GROUP, :].rearrange("(p t) k -> p (t k)", t=4)
+            if g == 0:
+                nc.sync.dma_start(out=t[:, 0:2048], in_=src[:, 0:2048])
+                nc.sync.dma_start(out=t[:, 2048:4096], in_=src[:, 2048:4096])
+            else:
+                nc.sync.dma_start(out=t[:], in_=src)
+            hraw.append(t)
+
+        load_group(0)
+        w2raw = consts.tile([P, 2048], BF16, name="w2raw")
+        nc.sync.dma_start(
+            out=w2raw[:].rearrange("p (a c) -> p a c", a=4),
+            in_=w2.rearrange("(a p) c -> p a c", p=P),
+        )
+        for g in range(1, 4):
+            load_group(g)
+        graw = consts.tile([P, 4], BF16, name="graw")
+        braw = consts.tile([P, 4], BF16, name="braw")
+        nc.scalar.dma_start(out=graw[:], in_=gamma.rearrange("(p t) -> p t", t=4))
+        nc.scalar.dma_start(out=braw[:], in_=beta.rearrange("(p t) -> p t", t=4))
+        nc.scalar.activation(
+            out=junk[:], in_=eps[:], func=(ACT.Abs_reciprocal_sqrt if USE_ARS else ACT.Sqrt)
+        )
+
+        hgrp = {}
+        hcodes = {}
+        hscales = {}
+
+        def transposes(g):
+            rawf = hraw[g][:].bitcast(F32)
+            grp = grps.tile([P, 4096], BF16, name="hgrp%d" % g, tag="grp", align_bytes=64)
+            grpf = grp[:].bitcast(F32)
+            for h in range(2):
+                for g2 in range(2):
+                    xt = psum.tile([P, 512], F32, name="xt%d_%d%d" % (g, h, g2), tag="xt")
+                    for u in range(2):
+                        for tt in range(2):
+                            col = (2 * h + tt) * 512 + 256 * g2 + u
+                            nc.tensor.transpose(
+                                xt[:, (2 * u + tt) * P : (2 * u + tt + 1) * P],
+                                rawf[:, col : col + 255 : 2],
+                                ident_f[:],
+                            )
+                    lo = g2 * 1024 + h * 512
+                    nc.scalar.copy(
+                        out=grpf[:, lo : lo + 512].rearrange("p (x u) -> p x u", u=2),
+                        in_=xt[:].rearrange("p (u x) -> p x u", u=2),
+                    )
+            hgrp[g] = grp
+
+        def quant_hops(g):
+            codes = hq.tile([P, 1024], U32, name="hc%d" % g, align_bytes=64)
+            scales = hq.tile([P, 1024], U8, name="hs%d" % g, align_bytes=64)
+            nc.vector.quantize_mx(out=codes[:].bitcast(FP8X4), scales=scales[:], in_=hgrp[g][:])
+            hcodes[g] = codes
+            hscales[g] = scales
+
+        wc = consts.tile([P, 1024], U32, name="wc", align_bytes=64)
+        ws = consts.tile([P, 1024], U8, name="ws", align_bytes=64)
+        stats = consts.tile([P, 4 * NG * 6], F32, name="stats")
+        zsrc = {}
+
+        def matmul1(g, tag, planes):
+            for T in planes:
+                acc = psum.tile([P, 512], F32, name="acc%d_%d" % (g, T), tag=tag)
+                for g2 in range(2):
+                    wsl = slice(g2 * 512 + T * P, g2 * 512 + (T + 1) * P)
+                    hsl = slice(g2 * 512, (g2 + 1) * 512)
+                    nc.tensor.matmul_mx(
+                        out=acc[:],
+                        lhsT=wc[:, wsl].bitcast(FP8X4),
+                        lhsT_scale=ws[:, wsl],
+                        rhs=hcodes[g][:, hsl].bitcast(FP8X4),
+                        rhs_scale=hscales[g][:, hsl],
+                        start=(g2 == 0),
+                        stop=(g2 == 1),
+                    )
+                zsrc[(g, T)] = acc[:]
+
+        def keep_and_stats(g):
+            banks = [zsrc[(g, T)] for T in range(4)]
+            if g not in IN_PSUM:
+                zt = zpool.tile([P, 512 * len(COPIED)], F32, name="z%d" % g)
+                for n, T in enumerate(COPIED):
+                    nc.scalar.copy(out=zt[:, n * 512 : (n + 1) * 512], in_=banks[T])
+                    zsrc[(g, T)] = zt[:, n * 512 : (n + 1) * 512]
+            for T in range(4):
+                k = (T * NG + g) * 6
+                nc.vector.bn_stats(out=stats[:, k : k + 6], in_=banks[T])
+
+        wgrp = grps.tile([P, 4096], BF16, name="wgrp", tag="grp", align_bytes=64)
+        for g2 in range(2):
+            sl = slice(g2 * 2048, (g2 + 1) * 2048)
+            nc.vector.tensor_copy(
+                out=wgrp[:, sl].rearrange("p (q m t) -> p q m t", q=4, t=4),
+                in_=wraw[:, sl].rearrange("p (t m q) -> p q m t", t=4, q=4),
+            )
+            ql = slice(g2 * 512, (g2 + 1) * 512)
+            nc.vector.quantize_mx(out=wc[:, ql].bitcast(FP8X4), scales=ws[:, ql], in_=wgrp[:, sl])
+
+        transposes(0)
+        quant_hops(0)
+
+        w2grp = consts.tile([P, 2048], BF16, name="w2grp", align_bytes=64)
+        w2words = w2raw[:].bitcast(F32)
+        for hh in range(2):
+            xw = psum.tile([P, 512], F32, name="xw%d" % hh, tag="acc")
+            for u in range(2):
+                for oo in range(2):
+                    col = (2 * hh + oo) * 256 + u
+                    nc.tensor.transpose(
+                        xw[:, (2 * u + oo) * P : (2 * u + oo + 1) * P],
+                        w2words[:, col : col + 255 : 2],
+                        ident_f[:],
+                    )
+            nc.scalar.copy(
+                out=w2grp[:].bitcast(F32)[:, hh * 512 : (hh + 1) * 512].rearrange("p (o u) -> p o u", u=2),
+                in_=xw[:].rearrange("p (u o) -> p o u", u=2),
+            )
+        gb = consts.tile([P, 8], F32, name="gb")
+        nc.scalar.copy(out=gb[:, 0:4], in_=graw[:])
+        nc.scalar.copy(out=gb[:, 4:8], in_=braw[:])
+        ngam = consts.tile([P, 4], F32, name="ngam")
+        nc.scalar.mul(out=ngam[:], in_=gb[:, 0:4], mul=-1.0)
+
+        b2bc = consts.tile([P, C], BF16, name="b2bc")
+        b2f = consts.tile([P, C], F32, name="b2f")
+        for g in range(4, NG):
+            load_group(g)
+        nc.sync.dma_start(out=b2bc[:], in_=b2.partition_broadcast(P))
+
+        ALL = (0, 1, 2, 3)
+        transposes(1)
+        quant_hops(1)
+        matmul1(0, "acc", ALL)
+        keep_and_stats(0)
+        transposes(2)
+        quant_hops(2)
+        for g in range(1, NG):
+            if g + 2 < NG:
+                transposes(g + 2)
+            matmul1(g, "xt" if g == NG - 1 else "acc", ALL)
+            keep_and_stats(g)
+            if g + 2 < NG:
+                quant_hops(g + 2)
+
+        mv = consts.tile([P, 8], F32, name="mv")
+        for T in range(4):
+            nc.vector.bn_aggr(out=mv[:, 2 * T : 2 * T + 2], in_=stats[:, T * NG * 6 : (T + 1) * NG * 6])
+        mvv = mv[:].rearrange("p (t s) -> p t s", s=2)
+        sc = consts.tile([P, 4], F32, name="sc")
+        bi = consts.tile([P, 4], F32, name="bi")
+        rstd = consts.tile([P, 4], F32, name="rstd")
+        nmg = consts.tile([P, 4], F32, name="nmg")
+        nc.vector.tensor_tensor(out=nmg[:], in0=mvv[:, :, 0], in1=ngam[:], op=ALU.mult)
+        if USE_ARS:
+            nc.scalar.activation(
+                out=rstd[:], in_=mvv[:, :, 1], func=ACT.Abs_reciprocal_sqrt, bias=eps[:, 0:1], scale=1.0
+            )
+        else:
+            std = consts.tile([P, 4], F32, name="std")
+            nc.scalar.activation(out=std[:], in_=mvv[:, :, 1], func=ACT.Sqrt, bias=eps[:, 0:1], scale=1.0)
+            nc.vector.reciprocal(out=rstd[:], in_=std[:])
+        for T in range(4):
+            nc.scalar.activation(
+                out=sc[:, T : T + 1], in_=rstd[:, T : T + 1], func=ACT.Identity, scale=gb[:, T : T + 1]
+            )
+            nc.scalar.activation(
+                out=bi[:, T : T + 1],
+                in_=rstd[:, T : T + 1],
+                func=ACT.Identity,
+                bias=gb[:, 4 + T : 5 + T],
+                scale=nmg[:, T : T + 1],
+            )
+
+        w2c = consts.tile([P, 512], U32, name="w2c", align_bytes=64)
+        w2s = consts.tile([P, 512], U8, name="w2s", align_bytes=64)
+        nc.vector.quantize_mx(out=w2c[:].bitcast(FP8X4), scales=w2s[:], in_=w2grp[:])
+        nc.vector.tensor_copy(out=b2f[:], in_=b2bc[:])
+
+        order = list(IN_PSUM) + [g for g in range(NG) if g not in IN_PSUM]
+        REDONE = tuple([T for T in ALL if T not in COPIED])
+        ycodes = {}
+        yscales = {}
+        yps = {}
+
+        def norm(g, on_vector):
+            yp = ypool.tile([P, 2048], BF16, name="yp%d" % g, tag="yp")
+            for T in range(4):
+                if on_vector:
+                    nc.vector.tensor_scalar(
+                        out=yp[:, T * 512 : (T + 1) * 512],
+                        in0=zsrc[(g, T)],
+                        scalar1=sc[:, T : T + 1],
+                        scalar2=bi[:, T : T + 1],
+                        op0=ALU.mult,
+                        op1=ALU.add,
+                    )
+                else:
+                    nc.scalar.activation(
+                        out=yp[:, T * 512 : (T + 1) * 512],
+                        in_=zsrc[(g, T)],
+                        func=ACT.Relu,
+                        bias=bi[:, T : T + 1],
+                        scale=sc[:, T : T + 1],
+                    )
+            yps[g] = yp
+
+        ygrps = {}
+
+        def regroup(g, relu_here):
+            ygrp = ypool.tile([P, 2048], BF16, name="ygrp%d" % g, tag="ygrp", align_bytes=64)
+            dstv = ygrp[:].rearrange("p (c i t) -> p c t i", i=4, t=4)
+            srcv = yps[g][:].rearrange("p (t c i) -> p c t i", t=4, i=4)
+            if relu_here:
+                nc.vector.tensor_scalar_max(out=dstv, in0=srcv, scalar1=0.0)
+            else:
+                if V_BLOCKS < 128:
+                    nc.scalar.copy(out=dstv[:, V_BLOCKS:128], in_=srcv[:, V_BLOCKS:128])
+                nc.vector.tensor_copy(out=dstv[:, 0:V_BLOCKS], in_=srcv[:, 0:V_BLOCKS])
+            ygrps[g] = ygrp
+
+        def quant_y(g):
+            ygrp = ygrps[g]
+            codes = ypool.tile([P, 512], U32, name="yc%d" % g, tag="yc", align_bytes=64)
+            scales = ypool.tile([P, 512], U8, name="ys%d" % g, tag="ys", align_bytes=64)
+            nc.vector.quantize_mx(out=codes[:].bitcast(FP8X4), scales=scales[:], in_=ygrp[:])
+            ycodes[g] = codes
+            yscales[g] = scales
+
+        obs = {}
+
+        def matmul2(g):
+            for t in range(4):
+                ob = psum.tile([P, 512], F32, name="ob%d_%d" % (g, t), tag="acc")
+                nc.tensor.matmul_mx(
+                    out=ob[:],
+                    lhsT=ycodes[g][:, t * P : (t + 1) * P].bitcast(FP8X4),
+                    lhsT_scale=yscales[g][:, t * P : (t + 1) * P],
+                    rhs=w2c[:].bitcast(FP8X4),
+                    rhs_scale=w2s[:],
+                    start=True,
+                    stop=True,
+                )
+                obs[(g, t)] = ob
+
+        osbs = {}
+
+        def finish(g, last, tiles):
+            if g not in osbs:
+                osbs[g] = opool.tile([P, 2048], F32, name="osb%d" % g, tag="osb")
+            osb = osbs[g]
+            dst = oflat[g * GROUP : (g + 1) * GROUP, :].rearrange("(r t) o -> r (t o)", t=4)
+            for t in tiles:
+                sl = slice(t * 512, (t + 1) * 512)
+                if t < S_FROM or last:
+                    nc.vector.tensor_tensor(out=osb[:, sl], in0=obs[(g, t)][:], in1=b2f[:], op=ALU.add)
+                else:
+                    nc.scalar.copy(out=osb[:, sl], in_=obs[(g, t)][:])
+                    nc.gpsimd.tensor_tensor(out=osb[:, sl], in0=osb[:, sl], in1=b2f[:], op=ALU.add)
+                nc.sync.dma_start(out=dst[:, sl], in_=osb[:, sl])
+
+        norm(order[0], False)
+        norm(order[1], True)
+        matmul1(order[2], "xt", REDONE)
+        matmul1(order[3], "xt", REDONE)
+        regroup(order[0], False)
+        regroup(order[1], True)
+        quant_y(order[0])
+        quant_y(order[1])
+        matmul2(order[0])
+        for j in range(2, NG + 2):
+            last = j - 2 == NG - 1
+            if j < NG:
+                norm(order[j], False)
+                if j + 2 < NG:
+                    matmul1(order[j + 2], "xt", REDONE)
+                regroup(order[j], False)
+                finish(order[j - 2], last, (0,))
+                quant_y(order[j])
+            else:
+                finish(order[j - 2], last, (0,))
+            if j - 1 < NG:
+                matmul2(order[j - 1])
+            finish(order[j - 2], last, (1, 2, 3))

@@ -64,14 +64,9 @@ def tile_ginconvfft_pb_t_kernel(tc, hops, weight, gamma, beta, w2, b2, out):
                 nc.sync.dma_start(out=t[:], in_=src)
             hraw.append(t)
 
-        load_group(0)
-        w2raw = consts.tile([P, 2048], BF16, name="w2raw")
-        nc.sync.dma_start(
-            out=w2raw[:].rearrange("p (a c) -> p a c", a=4),
-            in_=w2.rearrange("(a p) c -> p a c", p=P),
-        )
-        for g in range(1, 4):
+        for g in range(4):
             load_group(g)
+        w2raw = consts.tile([P, 2048], BF16, name="w2raw")
         graw = consts.tile([P, 4], BF16, name="graw")
         braw = consts.tile([P, 4], BF16, name="braw")
         nc.scalar.dma_start(out=graw[:], in_=gamma.rearrange("(p t) -> p t", t=4))
@@ -84,11 +79,12 @@ def tile_ginconvfft_pb_t_kernel(tc, hops, weight, gamma, beta, w2, b2, out):
         hcodes = {}
         hscales = {}
 
-        def transposes(g):
+        def transposes(g, halves):
             rawf = hraw[g][:].bitcast(F32)
-            grp = grps.tile([P, 4096], BF16, name="hgrp%d" % g, tag="grp", align_bytes=64)
-            grpf = grp[:].bitcast(F32)
-            for h in range(2):
+            if g not in hgrp:
+                hgrp[g] = grps.tile([P, 4096], BF16, name="hgrp%d" % g, tag="grp", align_bytes=64)
+            grpf = hgrp[g][:].bitcast(F32)
+            for h in halves:
                 for g2 in range(2):
                     xt = psum.tile([P, 512], F32, name="xt%d_%d%d" % (g, h, g2), tag="xt")
                     for u in range(2):
@@ -104,8 +100,6 @@ def tile_ginconvfft_pb_t_kernel(tc, hops, weight, gamma, beta, w2, b2, out):
                         out=grpf[:, lo : lo + 512].rearrange("p (x u) -> p x u", u=2),
                         in_=xt[:].rearrange("p (u x) -> p x u", u=2),
                     )
-            hgrp[g] = grp
-
         def quant_hops(g):
             codes = hq.tile([P, 1024], U32, name="hc%d" % g, align_bytes=64)
             scales = hq.tile([P, 1024], U8, name="hs%d" % g, align_bytes=64)
@@ -135,16 +129,15 @@ def tile_ginconvfft_pb_t_kernel(tc, hops, weight, gamma, beta, w2, b2, out):
                     )
                 zsrc[(g, T)] = acc[:]
 
-        def keep_and_stats(g):
-            banks = [zsrc[(g, T)] for T in range(4)]
-            if g not in IN_PSUM:
-                zt = zpool.tile([P, 512 * len(COPIED)], F32, name="z%d" % g)
-                for n, T in enumerate(COPIED):
-                    nc.scalar.copy(out=zt[:, n * 512 : (n + 1) * 512], in_=banks[T])
-                    zsrc[(g, T)] = zt[:, n * 512 : (n + 1) * 512]
-            for T in range(4):
+        def keep_and_stats(g, chunks):
+            for T in chunks:
+                bank = zsrc[(g, T)]
+                if g not in IN_PSUM and T in COPIED:
+                    zt = zpool.tile([P, 512], F32, name="z%d_%d" % (g, T))
+                    nc.scalar.copy(out=zt[:], in_=bank)
+                    zsrc[(g, T)] = zt[:]
                 k = (T * NG + g) * 6
-                nc.vector.bn_stats(out=stats[:, k : k + 6], in_=banks[T])
+                nc.vector.bn_stats(out=stats[:, k : k + 6], in_=bank)
 
         wgrp = grps.tile([P, 4096], BF16, name="wgrp", tag="grp", align_bytes=64)
         for g2 in range(2):
@@ -156,13 +149,33 @@ def tile_ginconvfft_pb_t_kernel(tc, hops, weight, gamma, beta, w2, b2, out):
             ql = slice(g2 * 512, (g2 + 1) * 512)
             nc.vector.quantize_mx(out=wc[:, ql].bitcast(FP8X4), scales=ws[:, ql], in_=wgrp[:, sl])
 
-        transposes(0)
+        ctx.enter_context(tc.manual_schedule(engines={mybir.EngineType.PE}))
+        transposes(0, (0, 1))
         quant_hops(0)
+        transposes(1, (0, 1))
+        quant_hops(1)
+
+        gb = consts.tile([P, 8], F32, name="gb")
+        nc.scalar.copy(out=gb[:, 0:4], in_=graw[:])
+        nc.scalar.copy(out=gb[:, 4:8], in_=braw[:])
+        ngam = consts.tile([P, 4], F32, name="ngam")
+        nc.scalar.mul(out=ngam[:], in_=gb[:, 0:4], mul=-1.0)
+
+        b2bc = consts.tile([P, C], BF16, name="b2bc")
+        b2f = consts.tile([P, C], F32, name="b2f")
+        for g in range(4, NG):
+            load_group(g)
+        nc.sync.dma_start(
+            out=w2raw[:].rearrange("p (a c) -> p a c", a=4),
+            in_=w2.rearrange("(a p) c -> p a c", p=P),
+        )
+        nc.sync.dma_start(out=b2bc[:], in_=b2.partition_broadcast(P))
 
         w2grp = consts.tile([P, 2048], BF16, name="w2grp", align_bytes=64)
         w2words = w2raw[:].bitcast(F32)
-        for hh in range(2):
-            xw = psum.tile([P, 512], F32, name="xw%d" % hh, tag="acc")
+
+        def transposes_w2(hh):
+            xw = psum.tile([P, 512], F32, name="xw%d" % hh, tag="xt")
             for u in range(2):
                 for oo in range(2):
                     col = (2 * hh + oo) * 256 + u
@@ -175,32 +188,24 @@ def tile_ginconvfft_pb_t_kernel(tc, hops, weight, gamma, beta, w2, b2, out):
                 out=w2grp[:].bitcast(F32)[:, hh * 512 : (hh + 1) * 512].rearrange("p (o u) -> p o u", u=2),
                 in_=xw[:].rearrange("p (u o) -> p o u", u=2),
             )
-        gb = consts.tile([P, 8], F32, name="gb")
-        nc.scalar.copy(out=gb[:, 0:4], in_=graw[:])
-        nc.scalar.copy(out=gb[:, 4:8], in_=braw[:])
-        ngam = consts.tile([P, 4], F32, name="ngam")
-        nc.scalar.mul(out=ngam[:], in_=gb[:, 0:4], mul=-1.0)
-
-        b2bc = consts.tile([P, C], BF16, name="b2bc")
-        b2f = consts.tile([P, C], F32, name="b2f")
-        for g in range(4, NG):
-            load_group(g)
-        nc.sync.dma_start(out=b2bc[:], in_=b2.partition_broadcast(P))
 
         ALL = (0, 1, 2, 3)
-        transposes(1)
-        quant_hops(1)
-        matmul1(0, "acc", ALL)
-        keep_and_stats(0)
-        transposes(2)
-        quant_hops(2)
-        for g in range(1, NG):
-            if g + 2 < NG:
-                transposes(g + 2)
-            matmul1(g, "xt" if g == NG - 1 else "acc", ALL)
-            keep_and_stats(g)
+        w2c = consts.tile([P, 512], U32, name="w2c", align_bytes=64)
+        w2s = consts.tile([P, 512], U8, name="w2s", align_bytes=64)
+        for g in range(NG):
+            for h in range(2):
+                chunks = ALL[2 * h : 2 * h + 2]
+                matmul1(g, "xt" if g == NG - 1 else "acc", chunks)
+                keep_and_stats(g, chunks)
+                if g + 2 < NG:
+                    transposes(g + 2, (h,))
+                elif g + 2 == NG:
+                    transposes_w2(h)
             if g + 2 < NG:
                 quant_hops(g + 2)
+            elif g + 2 == NG:
+                nc.vector.quantize_mx(out=w2c[:].bitcast(FP8X4), scales=w2s[:], in_=w2grp[:])
+                nc.vector.tensor_copy(out=b2f[:], in_=b2bc[:])
 
         mv = consts.tile([P, 8], F32, name="mv")
         for T in range(4):
@@ -230,11 +235,6 @@ def tile_ginconvfft_pb_t_kernel(tc, hops, weight, gamma, beta, w2, b2, out):
                 bias=gb[:, 4 + T : 5 + T],
                 scale=nmg[:, T : T + 1],
             )
-
-        w2c = consts.tile([P, 512], U32, name="w2c", align_bytes=64)
-        w2s = consts.tile([P, 512], U8, name="w2s", align_bytes=64)
-        nc.vector.quantize_mx(out=w2c[:].bitcast(FP8X4), scales=w2s[:], in_=w2grp[:])
-        nc.vector.tensor_copy(out=b2f[:], in_=b2bc[:])
 
         order = list(IN_PSUM) + [g for g in range(NG) if g not in IN_PSUM]
         REDONE = tuple([T for T in ALL if T not in COPIED])

@@ -21,9 +21,8 @@ IN_PSUM = (6, 7)
 COPIED = (0, 1)
 BN_EPS = 1e-5
 FLOPS = 2 * ROWS * K1 * C + 2 * ROWS * C * C
-V_BLOCKS = 96
+G_BLOCKS = 96
 USE_ARS = True
-S_FROM = 3
 
 
 def tile_ginconvfft_pb_t_kernel(tc, hops, weight, gamma, beta, w2, b2, out):
@@ -266,16 +265,28 @@ def tile_ginconvfft_pb_t_kernel(tc, hops, weight, gamma, beta, w2, b2, out):
 
         ygrps = {}
 
-        def regroup(g, relu_here):
+        def regroup(g, relu_here, on_gpsimd):
             ygrp = ypool.tile([P, 2048], BF16, name="ygrp%d" % g, tag="ygrp", align_bytes=64)
             dstv = ygrp[:].rearrange("p (c i t) -> p c t i", i=4, t=4)
             srcv = yps[g][:].rearrange("p (t c i) -> p c t i", t=4, i=4)
-            if relu_here:
+            dstg = ygrp[:].rearrange("p (r t) -> p r t", t=4)
+            srcg = yps[g][:].rearrange("p (t r) -> p r t", t=4)
+            if on_gpsimd:
+                for lo in range(0, 4 * G_BLOCKS, 128):
+                    nc.gpsimd.tensor_scalar(
+                        out=dstg[:, lo : lo + 128],
+                        in0=srcg[:, lo : lo + 128],
+                        scalar1=1.0,
+                        scalar2=0.0,
+                        op0=ALU.mult,
+                        op1=ALU.add,
+                    )
+                nc.scalar.copy(out=dstv[:, G_BLOCKS:128], in_=srcv[:, G_BLOCKS:128])
+            elif relu_here:
                 nc.vector.tensor_scalar_max(out=dstv, in0=srcv, scalar1=0.0)
             else:
-                if V_BLOCKS < 128:
-                    nc.scalar.copy(out=dstv[:, V_BLOCKS:128], in_=srcv[:, V_BLOCKS:128])
-                nc.vector.tensor_copy(out=dstv[:, 0:V_BLOCKS], in_=srcv[:, 0:V_BLOCKS])
+                nc.vector.tensor_copy(out=dstv[:, 0:G_BLOCKS], in_=srcv[:, 0:G_BLOCKS])
+                nc.scalar.copy(out=dstv[:, G_BLOCKS:128], in_=srcv[:, G_BLOCKS:128])
             ygrps[g] = ygrp
 
         def quant_y(g):
@@ -304,40 +315,34 @@ def tile_ginconvfft_pb_t_kernel(tc, hops, weight, gamma, beta, w2, b2, out):
 
         osbs = {}
 
-        def finish(g, last, tiles):
+        def finish(g, tiles):
             if g not in osbs:
                 osbs[g] = opool.tile([P, 2048], F32, name="osb%d" % g, tag="osb")
             osb = osbs[g]
             dst = oflat[g * GROUP : (g + 1) * GROUP, :].rearrange("(r t) o -> r (t o)", t=4)
             for t in tiles:
                 sl = slice(t * 512, (t + 1) * 512)
-                if t < S_FROM or last:
-                    nc.vector.tensor_tensor(out=osb[:, sl], in0=obs[(g, t)][:], in1=b2f[:], op=ALU.add)
-                else:
-                    nc.scalar.copy(out=osb[:, sl], in_=obs[(g, t)][:])
-                    nc.gpsimd.tensor_tensor(out=osb[:, sl], in0=osb[:, sl], in1=b2f[:], op=ALU.add)
+                nc.vector.tensor_tensor(out=osb[:, sl], in0=obs[(g, t)][:], in1=b2f[:], op=ALU.add)
                 nc.sync.dma_start(out=dst[:, sl], in_=osb[:, sl])
 
         norm(order[0], False)
         norm(order[1], True)
         matmul1(order[2], "xt", REDONE)
         matmul1(order[3], "xt", REDONE)
-        regroup(order[0], False)
-        regroup(order[1], True)
+        regroup(order[0], False, False)
+        regroup(order[1], True, False)
         quant_y(order[0])
-        quant_y(order[1])
         matmul2(order[0])
+        norm(order[2], False)
         for j in range(2, NG + 2):
-            last = j - 2 == NG - 1
             if j < NG:
-                norm(order[j], False)
-                if j + 2 < NG:
-                    matmul1(order[j + 2], "xt", REDONE)
-                regroup(order[j], False)
-                finish(order[j - 2], last, (0,))
-                quant_y(order[j])
-            else:
-                finish(order[j - 2], last, (0,))
+                regroup(order[j], False, j < NG - 1)
+            if j + 1 < NG:
+                norm(order[j + 1], False)
+            if j + 2 < NG:
+                matmul1(order[j + 2], "xt", REDONE)
+            finish(order[j - 2], (0, 1))
             if j - 1 < NG:
+                quant_y(order[j - 1])
                 matmul2(order[j - 1])
-            finish(order[j - 2], last, (1, 2, 3))
+            finish(order[j - 2], (2, 3))

@@ -22,7 +22,6 @@ COPIED = (0, 1)
 BN_EPS = 1e-5
 FLOPS = 2 * ROWS * K1 * C + 2 * ROWS * C * C
 G_BLOCKS = 96
-USE_ARS = True
 
 
 def tile_ginconvfft_pb_t_kernel(tc, hops, weight, gamma, beta, w2, b2, out):
@@ -38,6 +37,7 @@ def tile_ginconvfft_pb_t_kernel(tc, hops, weight, gamma, beta, w2, b2, out):
         hq = ctx.enter_context(tc.tile_pool(name="hq", bufs=1))
         zpool = ctx.enter_context(tc.tile_pool(name="zpool", bufs=1))
         ypool = ctx.enter_context(tc.tile_pool(name="ypool", bufs=3))
+        yppool = ctx.enter_context(tc.tile_pool(name="yppool", bufs=4))
         opool = ctx.enter_context(tc.tile_pool(name="opool", bufs=3))
         psum = ctx.enter_context(tc.psum_pool(name="psum", bufs=4))
 
@@ -71,7 +71,7 @@ def tile_ginconvfft_pb_t_kernel(tc, hops, weight, gamma, beta, w2, b2, out):
         nc.scalar.dma_start(out=graw[:], in_=gamma.rearrange("(p t) -> p t", t=4))
         nc.scalar.dma_start(out=braw[:], in_=beta.rearrange("(p t) -> p t", t=4))
         nc.scalar.activation(
-            out=junk[:], in_=eps[:], func=(ACT.Abs_reciprocal_sqrt if USE_ARS else ACT.Sqrt)
+            out=junk[:], in_=eps[:], func=ACT.Abs_reciprocal_sqrt
         )
 
         hgrp = {}
@@ -131,7 +131,7 @@ def tile_ginconvfft_pb_t_kernel(tc, hops, weight, gamma, beta, w2, b2, out):
         def keep_and_stats(g, chunks):
             for T in chunks:
                 bank = zsrc[(g, T)]
-                if g not in IN_PSUM and T in COPIED:
+                if T in COPIED:
                     zt = zpool.tile([P, 512], F32, name="z%d_%d" % (g, T))
                     nc.scalar.copy(out=zt[:], in_=bank)
                     zsrc[(g, T)] = zt[:]
@@ -189,12 +189,14 @@ def tile_ginconvfft_pb_t_kernel(tc, hops, weight, gamma, beta, w2, b2, out):
             )
 
         ALL = (0, 1, 2, 3)
+        EARLY = (0, 1, 2)
+        OFFLOAD = {NG - 3: (2,), NG - 2: (0,)}
         w2c = consts.tile([P, 512], U32, name="w2c", align_bytes=64)
         w2s = consts.tile([P, 512], U8, name="w2s", align_bytes=64)
         for g in range(NG):
             for h in range(2):
-                chunks = ALL[2 * h : 2 * h + 2]
-                matmul1(g, "xt" if g == NG - 1 else "acc", chunks)
+                chunks = EARLY[2 * h : 2 * h + 2]
+                matmul1(g, "xt" if g in IN_PSUM and h == 1 else "acc", chunks)
                 keep_and_stats(g, chunks)
                 if g + 2 < NG:
                     transposes(g + 2, (h,))
@@ -207,65 +209,58 @@ def tile_ginconvfft_pb_t_kernel(tc, hops, weight, gamma, beta, w2, b2, out):
                 nc.vector.tensor_copy(out=b2f[:], in_=b2bc[:])
 
         mv = consts.tile([P, 8], F32, name="mv")
-        for T in range(4):
-            nc.vector.bn_aggr(out=mv[:, 2 * T : 2 * T + 2], in_=stats[:, T * NG * 6 : (T + 1) * NG * 6])
         mvv = mv[:].rearrange("p (t s) -> p t s", s=2)
         sc = consts.tile([P, 4], F32, name="sc")
         bi = consts.tile([P, 4], F32, name="bi")
         rstd = consts.tile([P, 4], F32, name="rstd")
         nmg = consts.tile([P, 4], F32, name="nmg")
-        nc.vector.tensor_tensor(out=nmg[:], in0=mvv[:, :, 0], in1=ngam[:], op=ALU.mult)
-        if USE_ARS:
-            nc.scalar.activation(
-                out=rstd[:], in_=mvv[:, :, 1], func=ACT.Abs_reciprocal_sqrt, bias=eps[:, 0:1], scale=1.0
-            )
-        else:
-            std = consts.tile([P, 4], F32, name="std")
-            nc.scalar.activation(out=std[:], in_=mvv[:, :, 1], func=ACT.Sqrt, bias=eps[:, 0:1], scale=1.0)
-            nc.vector.reciprocal(out=rstd[:], in_=std[:])
-        for T in range(4):
-            nc.scalar.activation(
-                out=sc[:, T : T + 1], in_=rstd[:, T : T + 1], func=ACT.Identity, scale=gb[:, T : T + 1]
+
+        def scale_and_bias(first, end):
+            for T in range(first, end):
+                nc.vector.bn_aggr(out=mv[:, 2 * T : 2 * T + 2], in_=stats[:, T * NG * 6 : (T + 1) * NG * 6])
+            nc.vector.tensor_tensor(
+                out=nmg[:, first:end], in0=mvv[:, first:end, 0], in1=ngam[:, first:end], op=ALU.mult
             )
             nc.scalar.activation(
-                out=bi[:, T : T + 1],
-                in_=rstd[:, T : T + 1],
-                func=ACT.Identity,
-                bias=gb[:, 4 + T : 5 + T],
-                scale=nmg[:, T : T + 1],
+                out=rstd[:, first:end],
+                in_=mvv[:, first:end, 1],
+                func=ACT.Abs_reciprocal_sqrt,
+                bias=eps[:, 0:1],
+                scale=1.0,
             )
+            some = slice(first, end)
+            nc.vector.tensor_tensor(out=sc[:, some], in0=rstd[:, some], in1=gb[:, some], op=ALU.mult)
+            for T in range(first, end):
+                nc.vector.scalar_tensor_tensor(
+                    out=bi[:, T : T + 1],
+                    in0=nmg[:, T : T + 1],
+                    scalar=rstd[:, T : T + 1],
+                    in1=gb[:, 4 + T : 5 + T],
+                    op0=ALU.mult,
+                    op1=ALU.add,
+                )
 
         order = list(IN_PSUM) + [g for g in range(NG) if g not in IN_PSUM]
-        REDONE = tuple([T for T in ALL if T not in COPIED])
+        REDONE = (2, 3)
         ycodes = {}
         yscales = {}
         yps = {}
 
-        def norm(g, on_vector):
-            yp = ypool.tile([P, 2048], BF16, name="yp%d" % g, tag="yp")
-            for T in range(4):
-                if on_vector:
-                    nc.vector.tensor_scalar(
-                        out=yp[:, T * 512 : (T + 1) * 512],
-                        in0=zsrc[(g, T)],
-                        scalar1=sc[:, T : T + 1],
-                        scalar2=bi[:, T : T + 1],
-                        op0=ALU.mult,
-                        op1=ALU.add,
-                    )
-                else:
-                    nc.scalar.activation(
-                        out=yp[:, T * 512 : (T + 1) * 512],
-                        in_=zsrc[(g, T)],
-                        func=ACT.Relu,
-                        bias=bi[:, T : T + 1],
-                        scale=sc[:, T : T + 1],
-                    )
-            yps[g] = yp
+        def norm(g, chunks):
+            if g not in yps:
+                yps[g] = yppool.tile([P, 2048], BF16, name="yp%d" % g, tag="yp")
+            for T in chunks:
+                nc.scalar.activation(
+                    out=yps[g][:, T * 512 : (T + 1) * 512],
+                    in_=zsrc[(g, T)],
+                    func=ACT.Relu,
+                    bias=bi[:, T : T + 1],
+                    scale=sc[:, T : T + 1],
+                )
 
         ygrps = {}
 
-        def regroup(g, relu_here, on_gpsimd):
+        def regroup(g, on_gpsimd):
             ygrp = ypool.tile([P, 2048], BF16, name="ygrp%d" % g, tag="ygrp", align_bytes=64)
             dstv = ygrp[:].rearrange("p (c i t) -> p c t i", i=4, t=4)
             srcv = yps[g][:].rearrange("p (t c i) -> p c t i", t=4, i=4)
@@ -281,12 +276,9 @@ def tile_ginconvfft_pb_t_kernel(tc, hops, weight, gamma, beta, w2, b2, out):
                         op0=ALU.mult,
                         op1=ALU.add,
                     )
-                nc.scalar.copy(out=dstv[:, G_BLOCKS:128], in_=srcv[:, G_BLOCKS:128])
-            elif relu_here:
-                nc.vector.tensor_scalar_max(out=dstv, in0=srcv, scalar1=0.0)
             else:
                 nc.vector.tensor_copy(out=dstv[:, 0:G_BLOCKS], in_=srcv[:, 0:G_BLOCKS])
-                nc.scalar.copy(out=dstv[:, G_BLOCKS:128], in_=srcv[:, G_BLOCKS:128])
+            nc.scalar.copy(out=dstv[:, G_BLOCKS:128], in_=srcv[:, G_BLOCKS:128])
             ygrps[g] = ygrp
 
         def quant_y(g):
@@ -315,34 +307,46 @@ def tile_ginconvfft_pb_t_kernel(tc, hops, weight, gamma, beta, w2, b2, out):
 
         osbs = {}
 
-        def finish(g, tiles):
+        def finish(g, tiles, offloaded=()):
             if g not in osbs:
                 osbs[g] = opool.tile([P, 2048], F32, name="osb%d" % g, tag="osb")
             osb = osbs[g]
             dst = oflat[g * GROUP : (g + 1) * GROUP, :].rearrange("(r t) o -> r (t o)", t=4)
             for t in tiles:
                 sl = slice(t * 512, (t + 1) * 512)
-                nc.vector.tensor_tensor(out=osb[:, sl], in0=obs[(g, t)][:], in1=b2f[:], op=ALU.add)
+                if t in offloaded:
+                    nc.scalar.copy(out=osb[:, sl], in_=obs[(g, t)][:])
+                    nc.gpsimd.tensor_tensor(out=osb[:, sl], in0=osb[:, sl], in1=b2f[:], op=ALU.add)
+                else:
+                    nc.vector.tensor_tensor(out=osb[:, sl], in0=obs[(g, t)][:], in1=b2f[:], op=ALU.add)
                 nc.sync.dma_start(out=dst[:, sl], in_=osb[:, sl])
 
-        norm(order[0], False)
-        norm(order[1], True)
+        scale_and_bias(0, 3)
+        for g in range(NG):
+            matmul1(g, "xt" if g in IN_PSUM else "acc", (3,))
+            keep_and_stats(g, (3,))
+        norm(order[0], EARLY)
+        norm(order[1], EARLY)
         matmul1(order[2], "xt", REDONE)
-        matmul1(order[3], "xt", REDONE)
-        regroup(order[0], False, False)
-        regroup(order[1], True, False)
+        scale_and_bias(3, 4)
+        norm(order[0], (3,))
+        regroup(order[0], False)
+        norm(order[1], (3,))
         quant_y(order[0])
         matmul2(order[0])
-        norm(order[2], False)
+        matmul1(order[3], "xt", REDONE)
+        regroup(order[1], False)
+        norm(order[2], ALL)
         for j in range(2, NG + 2):
+            off = OFFLOAD.get(j - 2, ())
             if j < NG:
-                regroup(order[j], False, j < NG - 1)
+                regroup(order[j], j < NG - 1)
             if j + 1 < NG:
-                norm(order[j + 1], False)
-            if j + 2 < NG:
-                matmul1(order[j + 2], "xt", REDONE)
-            finish(order[j - 2], (0, 1))
+                norm(order[j + 1], ALL)
+            finish(order[j - 2], (0, 1), off)
             if j - 1 < NG:
                 quant_y(order[j - 1])
                 matmul2(order[j - 1])
-            finish(order[j - 2], (2, 3))
+            if j + 2 < NG:
+                matmul1(order[j + 2], "xt", REDONE)
+            finish(order[j - 2], (2, 3), off)

@@ -21,7 +21,6 @@ IN_PSUM = (6, 7)
 COPIED = (0, 1)
 BN_EPS = 1e-5
 FLOPS = 2 * ROWS * K1 * C + 2 * ROWS * C * C
-G_BLOCKS = 96
 
 
 def tile_ginconvfft_pb_t_kernel(tc, hops, weight, gamma, beta, w2, b2, out):
@@ -37,6 +36,7 @@ def tile_ginconvfft_pb_t_kernel(tc, hops, weight, gamma, beta, w2, b2, out):
         hq = ctx.enter_context(tc.tile_pool(name="hq", bufs=1))
         zpool = ctx.enter_context(tc.tile_pool(name="zpool", bufs=1))
         ypool = ctx.enter_context(tc.tile_pool(name="ypool", bufs=3))
+        ygpool = ctx.enter_context(tc.tile_pool(name="ygpool", bufs=1))
         yppool = ctx.enter_context(tc.tile_pool(name="yppool", bufs=4))
         opool = ctx.enter_context(tc.tile_pool(name="opool", bufs=3))
         psum = ctx.enter_context(tc.psum_pool(name="psum", bufs=4))
@@ -190,7 +190,6 @@ def tile_ginconvfft_pb_t_kernel(tc, hops, weight, gamma, beta, w2, b2, out):
 
         ALL = (0, 1, 2, 3)
         EARLY = (0, 1, 2)
-        OFFLOAD = {NG - 3: (2,), NG - 2: (0,)}
         w2c = consts.tile([P, 512], U32, name="w2c", align_bytes=64)
         w2s = consts.tile([P, 512], U8, name="w2s", align_bytes=64)
         for g in range(NG):
@@ -260,32 +259,41 @@ def tile_ginconvfft_pb_t_kernel(tc, hops, weight, gamma, beta, w2, b2, out):
 
         ygrps = {}
 
-        def regroup(g, on_gpsimd):
-            ygrp = ypool.tile([P, 2048], BF16, name="ygrp%d" % g, tag="ygrp", align_bytes=64)
-            dstv = ygrp[:].rearrange("p (c i t) -> p c t i", i=4, t=4)
-            srcv = yps[g][:].rearrange("p (t c i) -> p c t i", t=4, i=4)
-            dstg = ygrp[:].rearrange("p (r t) -> p r t", t=4)
-            srcg = yps[g][:].rearrange("p (t r) -> p r t", t=4)
+        def regroup_second(g):
+            second = ypool.tile([P, 1024], BF16, name="yh%d" % g, tag="yh", align_bytes=64)
+            nc.scalar.copy(
+                out=second[:].rearrange("p (c i t) -> p c t i", i=4, t=4),
+                in_=yps[g][:].rearrange("p (t c i) -> p c t i", t=4, i=4)[:, 64:128],
+            )
+            ygrps[g] = [None, second]
+
+        def regroup_first(g, on_gpsimd):
+            first = ygpool.tile([P, 1024], BF16, name="yg%d" % g, tag="yg", align_bytes=64)
+            rows = yps[g][:].rearrange("p (t r) -> p r t", t=4)
             if on_gpsimd:
-                for lo in range(0, 4 * G_BLOCKS, 128):
-                    nc.gpsimd.tensor_scalar(
-                        out=dstg[:, lo : lo + 128],
-                        in0=srcg[:, lo : lo + 128],
-                        scalar1=1.0,
-                        scalar2=0.0,
-                        op0=ALU.mult,
-                        op1=ALU.add,
-                    )
+                nc.gpsimd.tensor_scalar(
+                    out=first[:].rearrange("p (r t) -> p r t", t=4),
+                    in0=rows[:, 0:256],
+                    scalar1=1.0,
+                    scalar2=0.0,
+                    op0=ALU.mult,
+                    op1=ALU.add,
+                )
             else:
-                nc.vector.tensor_copy(out=dstv[:, 0:G_BLOCKS], in_=srcv[:, 0:G_BLOCKS])
-            nc.scalar.copy(out=dstv[:, G_BLOCKS:128], in_=srcv[:, G_BLOCKS:128])
-            ygrps[g] = ygrp
+                nc.vector.tensor_copy(
+                    out=first[:].rearrange("p (c i t) -> p c t i", i=4, t=4),
+                    in_=yps[g][:].rearrange("p (t c i) -> p c t i", t=4, i=4)[:, 0:64],
+                )
+            ygrps[g][0] = first
 
         def quant_y(g):
-            ygrp = ygrps[g]
             codes = ypool.tile([P, 512], U32, name="yc%d" % g, tag="yc", align_bytes=64)
             scales = ypool.tile([P, 512], U8, name="ys%d" % g, tag="ys", align_bytes=64)
-            nc.vector.quantize_mx(out=codes[:].bitcast(FP8X4), scales=scales[:], in_=ygrp[:])
+            for h in (1, 0):
+                words = slice(256 * h, 256 * h + 256)
+                nc.vector.quantize_mx(
+                    out=codes[:, words].bitcast(FP8X4), scales=scales[:, words], in_=ygrps[g][h][:]
+                )
             ycodes[g] = codes
             yscales[g] = scales
 
@@ -307,18 +315,14 @@ def tile_ginconvfft_pb_t_kernel(tc, hops, weight, gamma, beta, w2, b2, out):
 
         osbs = {}
 
-        def finish(g, tiles, offloaded=()):
+        def finish(g, tiles):
             if g not in osbs:
                 osbs[g] = opool.tile([P, 2048], F32, name="osb%d" % g, tag="osb")
             osb = osbs[g]
             dst = oflat[g * GROUP : (g + 1) * GROUP, :].rearrange("(r t) o -> r (t o)", t=4)
             for t in tiles:
                 sl = slice(t * 512, (t + 1) * 512)
-                if t in offloaded:
-                    nc.scalar.copy(out=osb[:, sl], in_=obs[(g, t)][:])
-                    nc.gpsimd.tensor_tensor(out=osb[:, sl], in0=osb[:, sl], in1=b2f[:], op=ALU.add)
-                else:
-                    nc.vector.tensor_tensor(out=osb[:, sl], in0=obs[(g, t)][:], in1=b2f[:], op=ALU.add)
+                nc.vector.tensor_tensor(out=osb[:, sl], in0=obs[(g, t)][:], in1=b2f[:], op=ALU.add)
                 nc.sync.dma_start(out=dst[:, sl], in_=osb[:, sl])
 
         scale_and_bias(0, 3)
@@ -330,23 +334,26 @@ def tile_ginconvfft_pb_t_kernel(tc, hops, weight, gamma, beta, w2, b2, out):
         matmul1(order[2], "xt", REDONE)
         scale_and_bias(3, 4)
         norm(order[0], (3,))
-        regroup(order[0], False)
+        regroup_second(order[0])
+        regroup_first(order[0], False)
         norm(order[1], (3,))
+        regroup_second(order[1])
         quant_y(order[0])
         matmul2(order[0])
         matmul1(order[3], "xt", REDONE)
-        regroup(order[1], False)
+        regroup_first(order[1], False)
         norm(order[2], ALL)
         for j in range(2, NG + 2):
-            off = OFFLOAD.get(j - 2, ())
             if j < NG:
-                regroup(order[j], j < NG - 1)
+                regroup_second(order[j])
             if j + 1 < NG:
                 norm(order[j + 1], ALL)
-            finish(order[j - 2], (0, 1), off)
+            finish(order[j - 2], (0, 1))
             if j - 1 < NG:
                 quant_y(order[j - 1])
                 matmul2(order[j - 1])
+            if j < NG:
+                regroup_first(order[j], j < NG - 1)
             if j + 2 < NG:
                 matmul1(order[j + 2], "xt", REDONE)
-            finish(order[j - 2], (2, 3), off)
+            finish(order[j - 2], (2, 3))

@@ -20,6 +20,7 @@ NG = ROWS // GROUP
 IN_PSUM = (6, 7)
 COPIED = (0, 1)
 BN_EPS = 1e-5
+SPLIT = 320
 FLOPS = 2 * ROWS * K1 * C + 2 * ROWS * C * C
 
 
@@ -260,20 +261,20 @@ def tile_ginconvfft_pb_t_kernel(tc, hops, weight, gamma, beta, w2, b2, out):
         ygrps = {}
 
         def regroup_second(g):
-            second = ypool.tile([P, 1024], BF16, name="yh%d" % g, tag="yh", align_bytes=64)
+            second = ypool.tile([P, 2048 - 4 * SPLIT], BF16, name="yh%d" % g, tag="yh", align_bytes=64)
             nc.scalar.copy(
                 out=second[:].rearrange("p (c i t) -> p c t i", i=4, t=4),
-                in_=yps[g][:].rearrange("p (t c i) -> p c t i", t=4, i=4)[:, 64:128],
+                in_=yps[g][:].rearrange("p (t c i) -> p c t i", t=4, i=4)[:, SPLIT // 4 : 128],
             )
             ygrps[g] = [None, second]
 
         def regroup_first(g, on_gpsimd):
-            first = ygpool.tile([P, 1024], BF16, name="yg%d" % g, tag="yg", align_bytes=64)
+            first = ygpool.tile([P, 4 * SPLIT], BF16, name="yg%d" % g, tag="yg", align_bytes=64)
             rows = yps[g][:].rearrange("p (t r) -> p r t", t=4)
             if on_gpsimd:
                 nc.gpsimd.tensor_scalar(
                     out=first[:].rearrange("p (r t) -> p r t", t=4),
-                    in0=rows[:, 0:256],
+                    in0=rows[:, 0:SPLIT],
                     scalar1=1.0,
                     scalar2=0.0,
                     op0=ALU.mult,
@@ -282,17 +283,19 @@ def tile_ginconvfft_pb_t_kernel(tc, hops, weight, gamma, beta, w2, b2, out):
             else:
                 nc.vector.tensor_copy(
                     out=first[:].rearrange("p (c i t) -> p c t i", i=4, t=4),
-                    in_=yps[g][:].rearrange("p (t c i) -> p c t i", t=4, i=4)[:, 0:64],
+                    in_=yps[g][:].rearrange("p (t c i) -> p c t i", t=4, i=4)[:, 0 : SPLIT // 4],
                 )
             ygrps[g][0] = first
 
         def quant_y(g):
             codes = ypool.tile([P, 512], U32, name="yc%d" % g, tag="yc", align_bytes=64)
             scales = ypool.tile([P, 512], U8, name="ys%d" % g, tag="ys", align_bytes=64)
-            for h in (1, 0):
-                words = slice(256 * h, 256 * h + 256)
+            for h, lo, hi in ((1, SPLIT, 448), (1, 448, 512), (0, 0, 256), (0, 256, SPLIT)):
+                base = SPLIT * h
                 nc.vector.quantize_mx(
-                    out=codes[:, words].bitcast(FP8X4), scales=scales[:, words], in_=ygrps[g][h][:]
+                    out=codes[:, lo:hi].bitcast(FP8X4),
+                    scales=scales[:, lo:hi],
+                    in_=ygrps[g][h][:, 4 * (lo - base) : 4 * (hi - base)],
                 )
             ycodes[g] = codes
             yscales[g] = scales

@@ -344,7 +344,7 @@ def tile_ginconvfft_pb_t_kernel(tc, hops, weight, gamma, beta, w2, b2, out):
         quant_y(order[0])
         matmul2(order[0])
         matmul1(order[3], "xt", REDONE)
-        regroup_first(order[1], False)
+        regroup_first(order[1], True)
         norm(order[2], ALL)
         for j in range(2, NG + 2):
             if j < NG:
@@ -356,7 +356,7 @@ def tile_ginconvfft_pb_t_kernel(tc, hops, weight, gamma, beta, w2, b2, out):
                 quant_y(order[j - 1])
                 matmul2(order[j - 1])
             if j < NG:
-                regroup_first(order[j], j < NG - 1)
+                regroup_first(order[j], True)
             if j + 2 < NG:
                 matmul1(order[j + 2], "xt", REDONE)
             finish(order[j - 2], (2, 3))

from contextlib import ExitStack

import concourse.mybir as mybir
from concourse.masks import make_identity

F32 = mybir.dt.float32
BF16 = mybir.dt.bfloat16
U32 = mybir.dt.uint32
U8 = mybir.dt.uint8
FP8X4 = mybir.dt.float8_e4m3fn_x4
ACT = mybir.ActivationFunctionType
ALU = mybir.AluOpType

P = 128
ROWS = 4096
K1 = 1024
C = 512
GROUP = 512
NG = ROWS // GROUP
IN_PSUM = (6, 7)
COPIED = (0, 1)
BN_EPS = 1e-5
SPLIT = 320
FLOPS = 2 * ROWS * K1 * C + 2 * ROWS * C * C


def tile_ginconvfft_pb_t_kernel(tc, hops, weight, gamma, beta, w2, b2, out):
    nc = tc.nc
    hflat = hops.rearrange("b n l m -> (b n) (l m)")
    wflat = weight.rearrange("l m c -> (l m) c")
    oflat = out.rearrange("b n o -> (b n) o")

    with ExitStack() as ctx:
        consts = ctx.enter_context(tc.tile_pool(name="consts", bufs=1))
        raws = ctx.enter_context(tc.tile_pool(name="raws", bufs=5))
        grps = ctx.enter_context(tc.tile_pool(name="grps", bufs=3))
        hq = ctx.enter_context(tc.tile_pool(name="hq", bufs=1))
        zpool = ctx.enter_context(tc.tile_pool(name="zpool", bufs=1))
        ypool = ctx.enter_context(tc.tile_pool(name="ypool", bufs=3))
        ygpool = ctx.enter_context(tc.tile_pool(name="ygpool", bufs=1))
        yppool = ctx.enter_context(tc.tile_pool(name="yppool", bufs=4))
        opool = ctx.enter_context(tc.tile_pool(name="opool", bufs=3))
        psum = ctx.enter_context(tc.psum_pool(name="psum", bufs=4))

        eps = consts.tile([P, 1], F32, name="eps")
        nc.vector.memset(eps[:], BN_EPS)
        junk = consts.tile([P, 1], F32, name="junk")
        ident_f = consts.tile([P, P], F32, name="ident_f")
        make_identity(nc, ident_f[:])

        wraw = raws.tile([P, 4096], BF16, name="wraw", tag="raw")
        wview = wflat.rearrange("(a p e) c -> p a (e c)", a=2, p=P, e=4)
        for g2 in range(2):
            nc.sync.dma_start(out=wraw[:, g2 * 2048 : (g2 + 1) * 2048], in_=wview[:, g2, :])
        hraw = []

        def load_group(g):
            t = raws.tile([P, 4096], BF16, name="hraw%d" % g, tag="raw")
            src = hflat[g * GROUP : (g + 1) * GROUP, :].rearrange("(p t) k -> p (t k)", t=4)
            if g == 0:
                nc.sync.dma_start(out=t[:, 0:2048], in_=src[:, 0:2048])
                nc.sync.dma_start(out=t[:, 2048:4096], in_=src[:, 2048:4096])
            else:
                nc.sync.dma_start(out=t[:], in_=src)
            hraw.append(t)

        for g in range(4):
            load_group(g)
        w2raw = consts.tile([P, 2048], BF16, name="w2raw")
        graw = consts.tile([P, 4], BF16, name="graw")
        braw = consts.tile([P, 4], BF16, name="braw")
        nc.scalar.dma_start(out=graw[:], in_=gamma.rearrange("(p t) -> p t", t=4))
        nc.scalar.dma_start(out=braw[:], in_=beta.rearrange("(p t) -> p t", t=4))
        nc.scalar.activation(
            out=junk[:], in_=eps[:], func=ACT.Abs_reciprocal_sqrt
        )

        hgrp = {}
        hcodes = {}
        hscales = {}

        def transposes(g, halves):
            rawf = hraw[g][:].bitcast(F32)
            if g not in hgrp:
                hgrp[g] = grps.tile([P, 4096], BF16, name="hgrp%d" % g, tag="grp", align_bytes=64)
            grpf = hgrp[g][:].bitcast(F32)
            for h in halves:
                for g2 in range(2):
                    xt = psum.tile([P, 512], F32, name="xt%d_%d%d" % (g, h, g2), tag="xt")
                    for u in range(2):
                        for tt in range(2):
                            col = (2 * h + tt) * 512 + 256 * g2 + u
                            nc.tensor.transpose(
                                xt[:, (2 * u + tt) * P : (2 * u + tt + 1) * P],
                                rawf[:, col : col + 255 : 2],
                                ident_f[:],
                            )
                    lo = g2 * 1024 + h * 512
                    nc.scalar.copy(
                        out=grpf[:, lo : lo + 512].rearrange("p (x u) -> p x u", u=2),
                        in_=xt[:].rearrange("p (u x) -> p x u", u=2),
                    )
        def quant_hops(g):
            codes = hq.tile([P, 1024], U32, name="hc%d" % g, align_bytes=64)
            scales = hq.tile([P, 1024], U8, name="hs%d" % g, align_bytes=64)
            nc.vector.quantize_mx(out=codes[:].bitcast(FP8X4), scales=scales[:], in_=hgrp[g][:])
            hcodes[g] = codes
            hscales[g] = scales

        wc = consts.tile([P, 1024], U32, name="wc", align_bytes=64)
        ws = consts.tile([P, 1024], U8, name="ws", align_bytes=64)
        stats = consts.tile([P, 4 * NG * 6], F32, name="stats")
        zsrc = {}

        def matmul1(g, tag, planes):
            for T in planes:
                acc = psum.tile([P, 512], F32, name="acc%d_%d" % (g, T), tag=tag)
                for g2 in range(2):
                    wsl = slice(g2 * 512 + T * P, g2 * 512 + (T + 1) * P)
                    hsl = slice(g2 * 512, (g2 + 1) * 512)
                    nc.tensor.matmul_mx(
                        out=acc[:],
                        lhsT=wc[:, wsl].bitcast(FP8X4),
                        lhsT_scale=ws[:, wsl],
                        rhs=hcodes[g][:, hsl].bitcast(FP8X4),
                        rhs_scale=hscales[g][:, hsl],
                        start=(g2 == 0),
                        stop=(g2 == 1),
                    )
                zsrc[(g, T)] = acc[:]

        def keep_and_stats(g, chunks):
            for T in chunks:
                bank = zsrc[(g, T)]
                if T in COPIED:
                    zt = zpool.tile([P, 512], F32, name="z%d_%d" % (g, T))
                    nc.scalar.copy(out=zt[:], in_=bank)
                    zsrc[(g, T)] = zt[:]
                k = (T * NG + g) * 6
                nc.vector.bn_stats(out=stats[:, k : k + 6], in_=bank)

        wgrp = grps.tile([P, 4096], BF16, name="wgrp", tag="grp", align_bytes=64)
        for g2 in range(2):
            sl = slice(g2 * 2048, (g2 + 1) * 2048)
            nc.vector.tensor_copy(
                out=wgrp[:, sl].rearrange("p (q m t) -> p q m t", q=4, t=4),
                in_=wraw[:, sl].rearrange("p (t m q) -> p q m t", t=4, q=4),
            )
            ql = slice(g2 * 512, (g2 + 1) * 512)
            nc.vector.quantize_mx(out=wc[:, ql].bitcast(FP8X4), scales=ws[:, ql], in_=wgrp[:, sl])

        ctx.enter_context(tc.manual_schedule(engines={mybir.EngineType.PE}))
        transposes(0, (0, 1))
        quant_hops(0)
        transposes(1, (0, 1))
        quant_hops(1)

        gb = consts.tile([P, 8], F32, name="gb")
        nc.scalar.copy(out=gb[:, 0:4], in_=graw[:])
        nc.scalar.copy(out=gb[:, 4:8], in_=braw[:])
        ngam = consts.tile([P, 4], F32, name="ngam")
        nc.scalar.mul(out=ngam[:], in_=gb[:, 0:4], mul=-1.0)

        b2bc = consts.tile([P, C], BF16, name="b2bc")
        b2f = consts.tile([P, C], F32, name="b2f")
        for g in range(4, NG):
            load_group(g)
        nc.sync.dma_start(
            out=w2raw[:].rearrange("p (a c) -> p a c", a=4),
            in_=w2.rearrange("(a p) c -> p a c", p=P),
        )
        nc.sync.dma_start(out=b2bc[:], in_=b2.partition_broadcast(P))

        w2grp = consts.tile([P, 2048], BF16, name="w2grp", align_bytes=64)
        w2words = w2raw[:].bitcast(F32)

        def transposes_w2(hh):
            xw = psum.tile([P, 512], F32, name="xw%d" % hh, tag="xt")
            for u in range(2):
                for oo in range(2):
                    col = (2 * hh + oo) * 256 + u
                    nc.tensor.transpose(
                        xw[:, (2 * u + oo) * P : (2 * u + oo + 1) * P],
                        w2words[:, col : col + 255 : 2],
                        ident_f[:],
                    )
            nc.scalar.copy(
                out=w2grp[:].bitcast(F32)[:, hh * 512 : (hh + 1) * 512].rearrange("p (o u) -> p o u", u=2),
                in_=xw[:].rearrange("p (u o) -> p o u", u=2),
            )

        ALL = (0, 1, 2, 3)
        EARLY = (0, 1, 2)
        w2c = consts.tile([P, 512], U32, name="w2c", align_bytes=64)
        w2s = consts.tile([P, 512], U8, name="w2s", align_bytes=64)
        for g in range(NG):
            for h in range(2):
                chunks = EARLY[2 * h : 2 * h + 2]
                matmul1(g, "xt" if g in IN_PSUM and h == 1 else "acc", chunks)
                keep_and_stats(g, chunks)
                if g + 2 < NG:
                    transposes(g + 2, (h,))
                elif g + 2 == NG:
                    transposes_w2(h)
            if g + 2 < NG:
                quant_hops(g + 2)
            elif g + 2 == NG:
                nc.vector.quantize_mx(out=w2c[:].bitcast(FP8X4), scales=w2s[:], in_=w2grp[:])
                nc.vector.tensor_copy(out=b2f[:], in_=b2bc[:])

        mv = consts.tile([P, 8], F32, name="mv")
        mvv = mv[:].rearrange("p (t s) -> p t s", s=2)
        sc = consts.tile([P, 4], F32, name="sc")
        bi = consts.tile([P, 4], F32, name="bi")
        rstd = consts.tile([P, 4], F32, name="rstd")
        nmg = consts.tile([P, 4], F32, name="nmg")

        def scale_and_bias(first, end):
            for T in range(first, end):
                nc.vector.bn_aggr(out=mv[:, 2 * T : 2 * T + 2], in_=stats[:, T * NG * 6 : (T + 1) * NG * 6])
            nc.vector.tensor_tensor(
                out=nmg[:, first:end], in0=mvv[:, first:end, 0], in1=ngam[:, first:end], op=ALU.mult
            )
            nc.scalar.activation(
                out=rstd[:, first:end],
                in_=mvv[:, first:end, 1],
                func=ACT.Abs_reciprocal_sqrt,
                bias=eps[:, 0:1],
                scale=1.0,
            )
            some = slice(first, end)
            nc.vector.tensor_tensor(out=sc[:, some], in0=rstd[:, some], in1=gb[:, some], op=ALU.mult)
            for T in range(first, end):
                nc.vector.scalar_tensor_tensor(
                    out=bi[:, T : T + 1],
                    in0=nmg[:, T : T + 1],
                    scalar=rstd[:, T : T + 1],
                    in1=gb[:, 4 + T : 5 + T],
                    op0=ALU.mult,
                    op1=ALU.add,
                )

        order = list(IN_PSUM) + [g for g in range(NG) if g not in IN_PSUM]
        REDONE = (2, 3)
        ycodes = {}
        yscales = {}
        yps = {}

        def norm(g, chunks):
            if g not in yps:
                yps[g] = yppool.tile([P, 2048], BF16, name="yp%d" % g, tag="yp")
            for T in chunks:
                nc.scalar.activation(
                    out=yps[g][:, T * 512 : (T + 1) * 512],
                    in_=zsrc[(g, T)],
                    func=ACT.Relu,
                    bias=bi[:, T : T + 1],
                    scale=sc[:, T : T + 1],
                )

        ygrps = {}

        def regroup_second(g):
            second = ypool.tile([P, 2048 - 4 * SPLIT], BF16, name="yh%d" % g, tag="yh", align_bytes=64)
            nc.scalar.copy(
                out=second[:].rearrange("p (c i t) -> p c t i", i=4, t=4),
                in_=yps[g][:].rearrange("p (t c i) -> p c t i", t=4, i=4)[:, SPLIT // 4 : 128],
            )
            ygrps[g] = [None, second]

        def regroup_first(g, on_gpsimd):
            first = ygpool.tile([P, 4 * SPLIT], BF16, name="yg%d" % g, tag="yg", align_bytes=64)
            rows = yps[g][:].rearrange("p (t r) -> p r t", t=4)
            if on_gpsimd:
                nc.gpsimd.tensor_scalar(
                    out=first[:].rearrange("p (r t) -> p r t", t=4),
                    in0=rows[:, 0:SPLIT],
                    scalar1=1.0,
                    scalar2=0.0,
                    op0=ALU.mult,
                    op1=ALU.add,
                )
            else:
                nc.vector.tensor_copy(
                    out=first[:].rearrange("p (c i t) -> p c t i", i=4, t=4),
                    in_=yps[g][:].rearrange("p (t c i) -> p c t i", t=4, i=4)[:, 0 : SPLIT // 4],
                )
            ygrps[g][0] = first

        def quant_y(g):
            codes = ypool.tile([P, 512], U32, name="yc%d" % g, tag="yc", align_bytes=64)
            scales = ypool.tile([P, 512], U8, name="ys%d" % g, tag="ys", align_bytes=64)
            for h, lo, hi in ((1, SPLIT, 448), (1, 448, 512), (0, 0, 256), (0, 256, SPLIT)):
                base = SPLIT * h
                nc.vector.quantize_mx(
                    out=codes[:, lo:hi].bitcast(FP8X4),
                    scales=scales[:, lo:hi],
                    in_=ygrps[g][h][:, 4 * (lo - base) : 4 * (hi - base)],
                )
            ycodes[g] = codes
            yscales[g] = scales

        obs = {}

        def matmul2(g):
            for t in range(4):
                ob = psum.tile([P, 512], F32, name="ob%d_%d" % (g, t), tag="acc")
                nc.tensor.matmul_mx(
                    out=ob[:],
                    lhsT=ycodes[g][:, t * P : (t + 1) * P].bitcast(FP8X4),
                    lhsT_scale=yscales[g][:, t * P : (t + 1) * P],
                    rhs=w2c[:].bitcast(FP8X4),
                    rhs_scale=w2s[:],
                    start=True,
                    stop=True,
                )
                obs[(g, t)] = ob

        osbs = {}

        def finish(g, tiles):
            if g not in osbs:
                osbs[g] = opool.tile([P, 2048], F32, name="osb%d" % g, tag="osb")
            osb = osbs[g]
            dst = oflat[g * GROUP : (g + 1) * GROUP, :].rearrange("(r t) o -> r (t o)", t=4)
            for t in tiles:
                sl = slice(t * 512, (t + 1) * 512)
                nc.vector.tensor_tensor(out=osb[:, sl], in0=obs[(g, t)][:], in1=b2f[:], op=ALU.add)
                nc.sync.dma_start(out=dst[:, sl], in_=osb[:, sl])

        scale_and_bias(0, 3)
        for g in range(NG):
            matmul1(g, "xt" if g in IN_PSUM else "acc", (3,))
            keep_and_stats(g, (3,))
        norm(order[0], EARLY)
        norm(order[1], EARLY)
        matmul1(order[2], "xt", REDONE)
        scale_and_bias(3, 4)
        norm(order[0], (3,))
        regroup_second(order[0])
        regroup_first(order[0], False)
        norm(order[1], (3,))
        regroup_second(order[1])
        quant_y(order[0])
        matmul2(order[0])
        matmul1(order[3], "xt", REDONE)
        regroup_first(order[1], True)
        norm(order[2], ALL)
        for j in range(2, NG + 2):
            if j < NG:
                regroup_second(order[j])
            if j + 1 < NG:
                norm(order[j + 1], ALL)
            finish(order[j - 2], (0, 1))
            if j - 1 < NG:
                quant_y(order[j - 1])
                matmul2(order[j - 1])
            if j < NG:
                regroup_first(order[j], True)
            if j + 2 < NG:
                matmul1(order[j + 2], "xt", REDONE)
            finish(order[j - 2], (2, 3))
